import numpy as np
import ml_dtypes


def mxq(x, axis, fmt="e4m3"):
    dtype, down = {"e4m3": (ml_dtypes.float8_e4m3fn, 7), "e5m2": (ml_dtypes.float8_e5m2, 14)}[fmt]
    v = np.moveaxis(np.asarray(x, np.float32).astype(ml_dtypes.bfloat16).astype(np.float64), axis, -1)
    blocks = v.reshape(v.shape[:-1] + (-1, 32))
    amax = np.abs(blocks).max(-1, keepdims=True)
    byte = np.maximum(np.where(amax > 0, np.frexp(amax)[1] - 1 + 127, 0) - down, 1)
    scale = np.exp2(byte - 127.0)
    codes = (blocks / scale).astype(np.float32).astype(dtype).astype(np.float64)
    return np.moveaxis((codes * scale).reshape(v.shape), -1, axis)


WIDE = False


def mx_kscale(k):
    if not WIDE:
        return np.ones(k)
    levels = np.array([10, -10, 5, -5, 0])
    a = np.random.permutation(np.resize(levels, k // 512 * 4)).reshape(k // 512, 4)
    idx = np.arange(k)
    return np.exp2(a[idx // 512, idx % 128 // 32])


BF16 = ml_dtypes.bfloat16


def bf(x):
    return np.asarray(x, np.float32).astype(BF16)


def f64(x):
    return np.asarray(x).astype(np.float64)


E2M1 = np.array([0.0, 0.5, 1.0, 1.5, 2.0, 3.0, 4.0, 6.0, -0.0, -0.5, -1.0, -1.5, -2.0, -3.0, -4.0, -6.0])


def pack_weight(w, fmt):
    k, n = w.shape
    w = f64(bf(w)).reshape(k // 32, 32, n)
    amax = np.abs(w).max(1)
    if fmt == "e4m3":
        byte = np.frexp(amax)[1] - 1 + 127 - 7
    else:
        mant, ex = np.frexp(amax / 6.0)
        byte = np.where(mant > 0.5, ex, ex - 1) + 127
    byte = np.clip(np.where(amax > 0, byte, 1), 1, 254)
    scaled = (w * np.exp2(127.0 - byte)[:, None, :]).reshape(k, n).astype(np.float32)
    by_word = np.ascontiguousarray(scaled.reshape(k // 512, 128, 4, n).transpose(0, 1, 3, 2))
    if fmt == "e4m3":
        words = by_word.astype(ml_dtypes.float8_e4m3fn).view(np.uint8)
    else:
        c = by_word.astype(ml_dtypes.float4_e2m1fn).view(np.uint8) & 0xF
        words = c[..., 0::2] | (c[..., 1::2] << 4)
    return np.ascontiguousarray(words), np.ascontiguousarray(byte.astype(np.uint8).reshape(k // 512, 16, n))


def unpack_weight(words, scales, fmt):
    g, p, n, _ = words.shape
    if fmt == "e4m3":
        vals = np.ascontiguousarray(words).view(ml_dtypes.float8_e4m3fn).astype(np.float64)
    else:
        nib = np.empty((g, p, n, 4), np.uint8)
        nib[..., 0::2] = words & 0xF
        nib[..., 1::2] = words >> 4
        vals = E2M1[nib]
    vals = vals * np.repeat(np.exp2(scales.astype(np.float64) - 127.0), 8, axis=1)[..., None]
    return vals.transpose(0, 1, 3, 2).reshape(g * 512, n)

def pack4(w):
    words, scales = pack_weight(w, "e2m1")
    return words.reshape(words.shape[0], 128, -1), scales


def unpack4(words, scales):
    return unpack_weight(words.reshape(words.shape[0], 128, -1, 2), scales, "e2m1")


B, S, D_IN, D_OUT = 3, 128, 16384, 512


def relative_shift(x):
    b, s, d = x.shape
    padded = np.concatenate([np.zeros((b, 1, d)), x], axis=1).reshape(s + 1, b, d)
    return padded[1:].reshape(b, s, d)


def setup_inputs():
    s = mx_kscale(D_IN)
    pos_embed = bf(np.random.standard_normal((B, S, D_IN)) * s)
    w = np.random.standard_normal((D_OUT, D_IN)) * 1.2 / np.sqrt(D_IN) / s[None, :]
    words, scales = pack4(np.ascontiguousarray(w.T))
    b_r = bf(np.random.standard_normal(D_OUT) * 0.3)
    return {"pos_embed": pos_embed,
            "W_r_words": words,
            "W_r_scales": scales,
            "b_r": b_r}


def reference(pos_embed, W_r_words, W_r_scales, b_r):
    shifted = relative_shift(f64(pos_embed))
    return (mxq(shifted, 2, "e4m3") @ unpack4(W_r_words, W_r_scales)) + f64(b_r)

@@ -1,0 +1,173 @@
+from contextlib import ExitStack
+
+import concourse.mybir as mybir
+from concourse.masks import make_identity
+
+BF16 = mybir.dt.bfloat16
+F32 = mybir.dt.float32
+I32 = mybir.dt.int32
+U32 = mybir.dt.uint32
+U8 = mybir.dt.uint8
+FP8X4 = mybir.dt.float8_e4m3fn_x4
+FP4X4 = mybir.dt.float4_e2m1fn_x4
+
+P = 128
+PACK = 4
+K_PASS = P * PACK
+ROWS = 384
+D_IN = 16384
+D_OUT = 512
+GROUPS = D_IN // K_PASS
+ROW_TILES = ROWS // P
+WORDS = K_PASS // 2
+PSUM_BANKS = 8
+
+FIRST_ROW = (2, 129, 256)
+
+STEP_GROUPS = 4
+CHUNKS = GROUPS // STEP_GROUPS
+BANK_GROUPS = 2
+STEP_BANKS = STEP_GROUPS // BANK_GROUPS
+SCALE_PARTS = 2
+PART_GROUPS = GROUPS // SCALE_PARTS
+
+FLOPS = 2 * ROWS * D_IN * D_OUT
+
+
+def tile_relativemultiheadattention_pa_k_kernel(tc, pos_embed, W_r_words, W_r_scales, b_r, out):
+    nc = tc.nc
+    x_rows = pos_embed.flatten_outer_dims()
+    out_rows = out.flatten_outer_dims()
+
+    with ExitStack() as ctx:
+        ctx.enter_context(tc.manual_schedule())
+        const = ctx.enter_context(tc.tile_pool(name="const", bufs=1))
+        x_pool = ctx.enter_context(tc.tile_pool(name="x", bufs=CHUNKS * ROW_TILES))
+        w_pool = ctx.enter_context(tc.tile_pool(name="w", bufs=CHUNKS))
+        plane_pool = ctx.enter_context(tc.tile_pool(name="plane", bufs=SCALE_PARTS))
+        grouped_pool = ctx.enter_context(tc.tile_pool(name="grouped", bufs=2 * STEP_BANKS))
+        code_pool = ctx.enter_context(tc.tile_pool(name="code", bufs=3 * STEP_BANKS))
+        result_pool = ctx.enter_context(tc.tile_pool(name="result", bufs=ROW_TILES))
+        sum_pool = ctx.enter_context(tc.psum_pool(name="sum", bufs=1))
+        bank_pool = ctx.enter_context(tc.psum_pool(name="bank", bufs=PSUM_BANKS - ROW_TILES))
+
+        planes = []
+        for part in range(SCALE_PARTS):
+            plane = plane_pool.tile([P, PART_GROUPS, D_OUT], U8, align_bytes=64, name="plane")
+            planes.append(plane)
+        nc.vector.memset(planes[0][:].rearrange("p g n -> p (g n)").bitcast(I32), 0)
+
+        bias_row = const.tile([P, D_OUT], BF16, name="bias_row")
+        ones = const.tile([P, P], BF16, name="ones")
+        nc.vector.memset(bias_row[:], 0.0)
+        nc.vector.memset(ones[:], 1.0)
+        nc.scalar.dma_start(out=bias_row[0:1, :], in_=b_r.unsqueeze(0))
+
+        selector = const.tile([P, ROW_TILES, P], F32, name="selector")
+        make_identity(nc, selector[:, 2, :])
+        nc.vector.memset(selector[:, 0:2, :], 0.0)
+        nc.vector.tensor_copy(out=selector[:, 0, 0:126], in_=selector[:, 2, 0:126])
+        nc.vector.tensor_copy(out=selector[:, 0, 127:128], in_=selector[:, 2, 126:127])
+        nc.vector.tensor_copy(out=selector[:, 1, 0:127], in_=selector[:, 2, 0:127])
+        for part in range(1, SCALE_PARTS):
+            nc.vector.memset(planes[part][:].rearrange("p g n -> p (g n)").bitcast(I32), 0)
+
+        def load_x(c, r):
+            x_tile = x_pool.tile([P, STEP_GROUPS * K_PASS], BF16, name="x_tile")
+            k0 = c * STEP_GROUPS * K_PASS
+            nc.sync.dma_start(
+                out=x_tile[:],
+                in_=x_rows[FIRST_ROW[r] : FIRST_ROW[r] + P, k0 : k0 + STEP_GROUPS * K_PASS],
+            )
+            return x_tile
+
+        def load_scales(part):
+            g0 = part * PART_GROUPS
+            for q in range(8):
+                first = 32 * (q // 4) + q % 4
+                nc.sync.dma_start(
+                    out=planes[part][first : P : 64, :, :].bitcast(I32),
+                    in_=W_r_scales[g0 : g0 + PART_GROUPS, q : 16 : 8, :].rearrange("g q n -> q g n").bitcast(I32),
+                )
+
+        def load_w(c):
+            w_tile = w_pool.tile([P, STEP_GROUPS, 2 * D_OUT], U8, align_bytes=64, name="w_tile")
+            g0 = c * STEP_GROUPS
+            nc.sync.dma_start(
+                out=w_tile[:].bitcast(I32),
+                in_=W_r_words[g0 : g0 + STEP_GROUPS].rearrange("g p b -> p g b").bitcast(I32),
+            )
+            return w_tile
+
+        x_tiles = {}
+        w_tiles = {}
+        for c in range(CHUNKS):
+            x_tiles[(c, 0)] = load_x(c, 0)
+            x_tiles[(c, 1)] = load_x(c, 1)
+            if (c * STEP_GROUPS) % PART_GROUPS == 0:
+                load_scales((c * STEP_GROUPS) // PART_GROUPS)
+            w_tiles[c] = load_w(c)
+            x_tiles[(c, 2)] = load_x(c, 2)
+
+        sums = []
+        for r in range(ROW_TILES):
+            total = sum_pool.tile([P, D_OUT], F32, name="sum%d" % r)
+            sums.append(total)
+
+        def prepare(step):
+            c, r = step
+            words = x_tiles[step][:].bitcast(F32)
+            quantised = []
+            for h in range(STEP_BANKS):
+                bank = bank_pool.tile([P, BANK_GROUPS, 2, P], F32, name="bank")
+                for i in range(BANK_GROUPS):
+                    w0 = (h * BANK_GROUPS + i) * WORDS
+                    for u in range(2):
+                        nc.tensor.transpose(bank[:, i, u, :], words[:, w0 + u : w0 + WORDS : 2], selector[:, r, :])
+                grouped = grouped_pool.tile([P, BANK_GROUPS * P * PACK], BF16, align_bytes=64, name="grouped")
+                nc.scalar.copy(
+                    out=grouped[:].bitcast(F32).rearrange("p (i j u) -> p i j u", i=BANK_GROUPS, u=2),
+                    in_=bank[:].rearrange("p i u j -> p i j u"),
+                )
+                codes = code_pool.tile([P, BANK_GROUPS * P], U32, align_bytes=64, name="codes")
+                scales = code_pool.tile([P, BANK_GROUPS * P], U8, align_bytes=64, name="scales")
+                nc.vector.quantize_mx(out=codes[:].bitcast(FP8X4), scales=scales[:], in_=grouped[:])
+                quantised.append((codes, scales))
+            return quantised
+
+        def multiply(step, quantised):
+            c, r = step
+            for in_chunk in range(STEP_GROUPS):
+                g = c * STEP_GROUPS + in_chunk
+                codes, scales = quantised[in_chunk // BANK_GROUPS]
+                i = in_chunk % BANK_GROUPS
+                nc.tensor.matmul_mx(
+                    out=sums[r][:],
+                    lhsT=codes[:, i * P : (i + 1) * P].bitcast(FP8X4),
+                    lhsT_scale=scales[:, i * P : (i + 1) * P],
+                    rhs=w_tiles[c][:, in_chunk, :].bitcast(FP4X4),
+                    rhs_scale=planes[g // PART_GROUPS][:, g % PART_GROUPS, :],
+                    start=(g == 0),
+                    stop=(g == GROUPS - 1),
+                )
+
+        def finish(r):
+            result = result_pool.tile([P, D_OUT], F32, name="result")
+            nc.vector.tensor_tensor(out=result[:], in0=sums[r][:], in1=bias_all[:], op=mybir.AluOpType.add)
+            nc.sync.dma_start(out=out_rows[r * P : (r + 1) * P, :], in_=result[:])
+
+        steps = [(c, r) for c in range(CHUNKS) for r in range(ROW_TILES)]
+
+        prepared = {steps[0]: prepare(steps[0])}
+
+        bias_bank = bank_pool.tile([P, D_OUT], F32, name="bank")
+        nc.tensor.matmul(bias_bank[:], lhsT=ones[:], rhs=bias_row[:], start=True, stop=True)
+        bias_all = const.tile([P, D_OUT], F32, name="bias_all")
+        nc.scalar.copy(out=bias_all[:], in_=bias_bank[:])
+
+        for s in range(len(steps)):
+            if s + 1 < len(steps):
+                prepared[steps[s + 1]] = prepare(steps[s + 1])
+            multiply(steps[s], prepared[steps[s]])
+            if steps[s][0] == CHUNKS - 1:
+                finish(steps[s][1])

@@ -45,6 +45,7 @@ def tile_relativemultiheadattention_pa_k_kernel(tc, pos_embed, W_r_words, W_r_sc
         x_pool = ctx.enter_context(tc.tile_pool(name="x", bufs=CHUNKS * ROW_TILES))
         w_pool = ctx.enter_context(tc.tile_pool(name="w", bufs=CHUNKS))
         plane_pool = ctx.enter_context(tc.tile_pool(name="plane", bufs=SCALE_PARTS))
+        sorted_pool = ctx.enter_context(tc.tile_pool(name="sorted", bufs=3 * STEP_BANKS))
         grouped_pool = ctx.enter_context(tc.tile_pool(name="grouped", bufs=2 * STEP_BANKS))
         code_pool = ctx.enter_context(tc.tile_pool(name="code", bufs=3 * STEP_BANKS))
         result_pool = ctx.enter_context(tc.tile_pool(name="result", bufs=ROW_TILES))
@@ -114,16 +115,27 @@ def tile_relativemultiheadattention_pa_k_kernel(tc, pos_embed, W_r_words, W_r_sc
             total = sum_pool.tile([P, D_OUT], F32, name="sum%d" % r)
             sums.append(total)
 
-        def prepare(step):
-            c, r = step
+        def sort_words(step):
             words = x_tiles[step][:].bitcast(F32)
+            sorted_banks = []
+            for h in range(STEP_BANKS):
+                in_order = sorted_pool.tile([P, BANK_GROUPS, 2, P], F32, name="in_order")
+                w0 = h * BANK_GROUPS * WORDS
+                nc.vector.tensor_copy(
+                    out=in_order[:],
+                    in_=words[:, w0 : w0 + BANK_GROUPS * WORDS].rearrange("r (i p u) -> r i u p", i=BANK_GROUPS, u=2),
+                )
+                sorted_banks.append(in_order)
+            return sorted_banks
+
+        def prepare(step, sorted_banks):
+            r = step[1]
             quantised = []
             for h in range(STEP_BANKS):
                 bank = bank_pool.tile([P, BANK_GROUPS, 2, P], F32, name="bank")
                 for i in range(BANK_GROUPS):
-                    w0 = (h * BANK_GROUPS + i) * WORDS
                     for u in range(2):
-                        nc.tensor.transpose(bank[:, i, u, :], words[:, w0 + u : w0 + WORDS : 2], selector[:, r, :])
+                        nc.tensor.transpose(bank[:, i, u, :], sorted_banks[h][:, i, u, :], selector[:, r, :])
                 grouped = grouped_pool.tile([P, BANK_GROUPS * P * PACK], BF16, align_bytes=64, name="grouped")
                 nc.scalar.copy(
                     out=grouped[:].bitcast(F32).rearrange("p (i j u) -> p i j u", i=BANK_GROUPS, u=2),
@@ -158,7 +170,8 @@ def tile_relativemultiheadattention_pa_k_kernel(tc, pos_embed, W_r_words, W_r_sc
 
         steps = [(c, r) for c in range(CHUNKS) for r in range(ROW_TILES)]
 
-        prepared = {steps[0]: prepare(steps[0])}
+        in_order_of = {steps[0]: sort_words(steps[0]), steps[1]: sort_words(steps[1])}
+        prepared = {steps[0]: prepare(steps[0], in_order_of[steps[0]])}
 
         bias_bank = bank_pool.tile([P, D_OUT], F32, name="bank")
         nc.tensor.matmul(bias_bank[:], lhsT=ones[:], rhs=bias_row[:], start=True, stop=True)
@@ -166,8 +179,10 @@ def tile_relativemultiheadattention_pa_k_kernel(tc, pos_embed, W_r_words, W_r_sc
         nc.scalar.copy(out=bias_all[:], in_=bias_bank[:])
 
         for s in range(len(steps)):
+            if s + 2 < len(steps):
+                in_order_of[steps[s + 2]] = sort_words(steps[s + 2])
             if s + 1 < len(steps):
-                prepared[steps[s + 1]] = prepare(steps[s + 1])
+                prepared[steps[s + 1]] = prepare(steps[s + 1], in_order_of[steps[s + 1]])
             multiply(steps[s], prepared[steps[s]])
             if steps[s][0] == CHUNKS - 1:
                 finish(steps[s][1])

@@ -19,6 +19,7 @@ D_IN = 16384
 D_OUT = 512
 GROUPS = D_IN // K_PASS
 ROW_TILES = ROWS // P
+LAST = ROW_TILES - 1
 WORDS = K_PASS // 2
 PSUM_BANKS = 8
 
@@ -28,8 +29,8 @@ STEP_GROUPS = 4
 CHUNKS = GROUPS // STEP_GROUPS
 BANK_GROUPS = 2
 STEP_BANKS = STEP_GROUPS // BANK_GROUPS
-SCALE_PARTS = 2
-PART_GROUPS = GROUPS // SCALE_PARTS
+PART_GROUPS = 8
+SCALE_PARTS = GROUPS // PART_GROUPS
 
 FLOPS = 2 * ROWS * D_IN * D_OUT
 
@@ -45,9 +46,9 @@ def tile_relativemultiheadattention_pa_k_kernel(tc, pos_embed, W_r_words, W_r_sc
         x_pool = ctx.enter_context(tc.tile_pool(name="x", bufs=CHUNKS * ROW_TILES))
         w_pool = ctx.enter_context(tc.tile_pool(name="w", bufs=CHUNKS))
         plane_pool = ctx.enter_context(tc.tile_pool(name="plane", bufs=SCALE_PARTS))
-        sorted_pool = ctx.enter_context(tc.tile_pool(name="sorted", bufs=3 * STEP_BANKS))
-        grouped_pool = ctx.enter_context(tc.tile_pool(name="grouped", bufs=2 * STEP_BANKS))
-        code_pool = ctx.enter_context(tc.tile_pool(name="code", bufs=3 * STEP_BANKS))
+        sorted_pool = ctx.enter_context(tc.tile_pool(name="sorted", bufs=2 * ROW_TILES))
+        grouped_pool = ctx.enter_context(tc.tile_pool(name="grouped", bufs=ROW_TILES * STEP_BANKS))
+        code_pool = ctx.enter_context(tc.tile_pool(name="code", bufs=2 * ROW_TILES * STEP_BANKS))
         result_pool = ctx.enter_context(tc.tile_pool(name="result", bufs=ROW_TILES))
         sum_pool = ctx.enter_context(tc.psum_pool(name="sum", bufs=1))
         bank_pool = ctx.enter_context(tc.psum_pool(name="bank", bufs=PSUM_BANKS - ROW_TILES))
@@ -55,14 +56,8 @@ def tile_relativemultiheadattention_pa_k_kernel(tc, pos_embed, W_r_words, W_r_sc
         planes = []
         for part in range(SCALE_PARTS):
             plane = plane_pool.tile([P, PART_GROUPS, D_OUT], U8, align_bytes=64, name="plane")
+            nc.vector.memset(plane[:].rearrange("p g n -> p (g n)").bitcast(I32), 0)
             planes.append(plane)
-        nc.vector.memset(planes[0][:].rearrange("p g n -> p (g n)").bitcast(I32), 0)
-
-        bias_row = const.tile([P, D_OUT], BF16, name="bias_row")
-        ones = const.tile([P, P], BF16, name="ones")
-        nc.vector.memset(bias_row[:], 0.0)
-        nc.vector.memset(ones[:], 1.0)
-        nc.scalar.dma_start(out=bias_row[0:1, :], in_=b_r.unsqueeze(0))
 
         selector = const.tile([P, ROW_TILES, P], F32, name="selector")
         make_identity(nc, selector[:, 2, :])
@@ -70,8 +65,12 @@ def tile_relativemultiheadattention_pa_k_kernel(tc, pos_embed, W_r_words, W_r_sc
         nc.vector.tensor_copy(out=selector[:, 0, 0:126], in_=selector[:, 2, 0:126])
         nc.vector.tensor_copy(out=selector[:, 0, 127:128], in_=selector[:, 2, 126:127])
         nc.vector.tensor_copy(out=selector[:, 1, 0:127], in_=selector[:, 2, 0:127])
-        for part in range(1, SCALE_PARTS):
-            nc.vector.memset(planes[part][:].rearrange("p g n -> p (g n)").bitcast(I32), 0)
+
+        bias_row = const.tile([P, D_OUT], BF16, name="bias_row")
+        ones = const.tile([P, P], BF16, name="ones")
+        nc.vector.memset(bias_row[:], 0.0)
+        nc.vector.memset(ones[:], 1.0)
+        nc.scalar.dma_start(out=bias_row[0:1, :], in_=b_r.unsqueeze(0))
 
         def load_x(c, r):
             x_tile = x_pool.tile([P, STEP_GROUPS * K_PASS], BF16, name="x_tile")
@@ -84,11 +83,10 @@ def tile_relativemultiheadattention_pa_k_kernel(tc, pos_embed, W_r_words, W_r_sc
 
         def load_scales(part):
             g0 = part * PART_GROUPS
-            for q in range(8):
-                first = 32 * (q // 4) + q % 4
+            for t in range(4):
                 nc.sync.dma_start(
-                    out=planes[part][first : P : 64, :, :].bitcast(I32),
-                    in_=W_r_scales[g0 : g0 + PART_GROUPS, q : 16 : 8, :].rearrange("g q n -> q g n").bitcast(I32),
+                    out=planes[part][t : P : 32, :, :].bitcast(I32),
+                    in_=W_r_scales[g0 : g0 + PART_GROUPS, t : 16 : 4, :].rearrange("g q n -> q g n").bitcast(I32),
                 )
 
         def load_w(c):
@@ -103,12 +101,11 @@ def tile_relativemultiheadattention_pa_k_kernel(tc, pos_embed, W_r_words, W_r_sc
         x_tiles = {}
         w_tiles = {}
         for c in range(CHUNKS):
-            x_tiles[(c, 0)] = load_x(c, 0)
-            x_tiles[(c, 1)] = load_x(c, 1)
+            for r in range(ROW_TILES):
+                x_tiles[(c, r)] = load_x(c, r)
             if (c * STEP_GROUPS) % PART_GROUPS == 0:
                 load_scales((c * STEP_GROUPS) // PART_GROUPS)
             w_tiles[c] = load_w(c)
-            x_tiles[(c, 2)] = load_x(c, 2)
 
         sums = []
         for r in range(ROW_TILES):
@@ -116,42 +113,43 @@ def tile_relativemultiheadattention_pa_k_kernel(tc, pos_embed, W_r_words, W_r_sc
             sums.append(total)
 
         def sort_words(step):
-            words = x_tiles[step][:].bitcast(F32)
-            sorted_banks = []
-            for h in range(STEP_BANKS):
-                in_order = sorted_pool.tile([P, BANK_GROUPS, 2, P], F32, name="in_order")
-                w0 = h * BANK_GROUPS * WORDS
-                nc.vector.tensor_copy(
-                    out=in_order[:],
-                    in_=words[:, w0 : w0 + BANK_GROUPS * WORDS].rearrange("r (i p u) -> r i u p", i=BANK_GROUPS, u=2),
-                )
-                sorted_banks.append(in_order)
-            return sorted_banks
+            in_order = sorted_pool.tile([P, STEP_GROUPS, 2, P], F32, name="in_order")
+            nc.vector.tensor_copy(
+                out=in_order[:].rearrange("r i u p -> r i p u"),
+                in_=x_tiles[step][:].bitcast(F32).rearrange("r (i p u) -> r i p u", i=STEP_GROUPS, u=2),
+            )
+            return in_order
 
-        def prepare(step, sorted_banks):
+        def transpose_step(step, in_order):
             r = step[1]
-            quantised = []
+            grouped_banks = []
             for h in range(STEP_BANKS):
                 bank = bank_pool.tile([P, BANK_GROUPS, 2, P], F32, name="bank")
                 for i in range(BANK_GROUPS):
                     for u in range(2):
-                        nc.tensor.transpose(bank[:, i, u, :], sorted_banks[h][:, i, u, :], selector[:, r, :])
+                        nc.tensor.transpose(bank[:, i, u, :], in_order[:, h * BANK_GROUPS + i, u, :], selector[:, r, :])
                 grouped = grouped_pool.tile([P, BANK_GROUPS * P * PACK], BF16, align_bytes=64, name="grouped")
                 nc.scalar.copy(
                     out=grouped[:].bitcast(F32).rearrange("p (i j u) -> p i j u", i=BANK_GROUPS, u=2),
                     in_=bank[:].rearrange("p i u j -> p i j u"),
                 )
+                grouped_banks.append(grouped)
+            return grouped_banks
+
+        def quantise_step(grouped_banks):
+            quantised_banks = []
+            for grouped in grouped_banks:
                 codes = code_pool.tile([P, BANK_GROUPS * P], U32, align_bytes=64, name="codes")
                 scales = code_pool.tile([P, BANK_GROUPS * P], U8, align_bytes=64, name="scales")
                 nc.vector.quantize_mx(out=codes[:].bitcast(FP8X4), scales=scales[:], in_=grouped[:])
-                quantised.append((codes, scales))
-            return quantised
+                quantised_banks.append((codes, scales))
+            return quantised_banks
 
-        def multiply(step, quantised):
+        def multiply(step, quantised_banks):
             c, r = step
             for in_chunk in range(STEP_GROUPS):
                 g = c * STEP_GROUPS + in_chunk
-                codes, scales = quantised[in_chunk // BANK_GROUPS]
+                codes, scales = quantised_banks[in_chunk // BANK_GROUPS]
                 i = in_chunk % BANK_GROUPS
                 nc.tensor.matmul_mx(
                     out=sums[r][:],
@@ -162,27 +160,31 @@ def tile_relativemultiheadattention_pa_k_kernel(tc, pos_embed, W_r_words, W_r_sc
                     start=(g == 0),
                     stop=(g == GROUPS - 1),
                 )
+            if c == CHUNKS - 1:
+                result = result_pool.tile([P, D_OUT], F32, name="result")
+                nc.vector.tensor_tensor(out=result[:], in0=sums[r][:], in1=bias_all[:], op=mybir.AluOpType.add)
+                nc.sync.dma_start(out=out_rows[r * P : (r + 1) * P, :], in_=result[:])
 
-        def finish(r):
-            result = result_pool.tile([P, D_OUT], F32, name="result")
-            nc.vector.tensor_tensor(out=result[:], in0=sums[r][:], in1=bias_all[:], op=mybir.AluOpType.add)
-            nc.sync.dma_start(out=out_rows[r * P : (r + 1) * P, :], in_=result[:])
-
-        steps = [(c, r) for c in range(CHUNKS) for r in range(ROW_TILES)]
-
-        in_order_of = {steps[0]: sort_words(steps[0]), steps[1]: sort_words(steps[1])}
-        prepared = {steps[0]: prepare(steps[0], in_order_of[steps[0]])}
-
-        bias_bank = bank_pool.tile([P, D_OUT], F32, name="bank")
-        nc.tensor.matmul(bias_bank[:], lhsT=ones[:], rhs=bias_row[:], start=True, stop=True)
-        bias_all = const.tile([P, D_OUT], F32, name="bias_all")
-        nc.scalar.copy(out=bias_all[:], in_=bias_bank[:])
-
-        for s in range(len(steps)):
-            if s + 2 < len(steps):
-                in_order_of[steps[s + 2]] = sort_words(steps[s + 2])
-            if s + 1 < len(steps):
-                prepared[steps[s + 1]] = prepare(steps[s + 1], in_order_of[steps[s + 1]])
-            multiply(steps[s], prepared[steps[s]])
-            if steps[s][0] == CHUNKS - 1:
-                finish(steps[s][1])
+        in_order_of = {}
+        quantised = {}
+        for r in range(ROW_TILES):
+            in_order_of[(0, r)] = sort_words((0, r))
+        for c in range(CHUNKS):
+            for r in range(ROW_TILES):
+                grouped_banks = transpose_step((c, r), in_order_of[(c, r)])
+                if r < LAST:
+                    quantised[(c, r)] = quantise_step(grouped_banks)
+            if c + 1 < CHUNKS:
+                for r in range(ROW_TILES):
+                    in_order_of[(c + 1, r)] = sort_words((c + 1, r))
+            quantised[(c, LAST)] = quantise_step(grouped_banks)
+            if c == 0:
+                bias_bank = bank_pool.tile([P, D_OUT], F32, name="bank")
+                nc.tensor.matmul(bias_bank[:], lhsT=ones[:], rhs=bias_row[:], start=True, stop=True)
+                bias_all = const.tile([P, D_OUT], F32, name="bias_all")
+                nc.scalar.copy(out=bias_all[:], in_=bias_bank[:])
+            else:
+                multiply((c - 1, LAST), quantised[(c - 1, LAST)])
+            for r in range(LAST):
+                multiply((c, r), quantised[(c, r)])
+        multiply((CHUNKS - 1, LAST), quantised[(CHUNKS - 1, LAST)])

@@ -29,8 +29,12 @@ STEP_GROUPS = 4
 CHUNKS = GROUPS // STEP_GROUPS
 BANK_GROUPS = 2
 STEP_BANKS = STEP_GROUPS // BANK_GROUPS
-PART_GROUPS = 8
-SCALE_PARTS = GROUPS // PART_GROUPS
+PART_GROUPS = (4, 8, 8, 8, 4)
+SCALE_PARTS = len(PART_GROUPS)
+FIRST_OF_PART = tuple(sum(PART_GROUPS[:part]) for part in range(SCALE_PARTS))
+PART_OF_GROUP = tuple(part for part in range(SCALE_PARTS) for g in range(PART_GROUPS[part]))
+HALF = D_OUT // 2
+LAST_SUMMED = (GROUPS - 1, GROUPS - 1, GROUPS - STEP_GROUPS - 1)
 
 FLOPS = 2 * ROWS * D_IN * D_OUT
 
@@ -55,7 +59,7 @@ def tile_relativemultiheadattention_pa_k_kernel(tc, pos_embed, W_r_words, W_r_sc
 
         planes = []
         for part in range(SCALE_PARTS):
-            plane = plane_pool.tile([P, PART_GROUPS, D_OUT], U8, align_bytes=64, name="plane")
+            plane = plane_pool.tile([P, PART_GROUPS[part], D_OUT], U8, align_bytes=64, name="plane")
             nc.vector.memset(plane[:].rearrange("p g n -> p (g n)").bitcast(I32), 0)
             planes.append(plane)
 
@@ -70,7 +74,6 @@ def tile_relativemultiheadattention_pa_k_kernel(tc, pos_embed, W_r_words, W_r_sc
         ones = const.tile([P, P], BF16, name="ones")
         nc.vector.memset(bias_row[:], 0.0)
         nc.vector.memset(ones[:], 1.0)
-        nc.scalar.dma_start(out=bias_row[0:1, :], in_=b_r.unsqueeze(0))
 
         def load_x(c, r):
             x_tile = x_pool.tile([P, STEP_GROUPS * K_PASS], BF16, name="x_tile")
@@ -82,11 +85,11 @@ def tile_relativemultiheadattention_pa_k_kernel(tc, pos_embed, W_r_words, W_r_sc
             return x_tile
 
         def load_scales(part):
-            g0 = part * PART_GROUPS
+            g0 = FIRST_OF_PART[part]
             for t in range(4):
                 nc.sync.dma_start(
                     out=planes[part][t : P : 32, :, :].bitcast(I32),
-                    in_=W_r_scales[g0 : g0 + PART_GROUPS, t : 16 : 4, :].rearrange("g q n -> q g n").bitcast(I32),
+                    in_=W_r_scales[g0 : g0 + PART_GROUPS[part], t : 16 : 4, :].rearrange("g q n -> q g n").bitcast(I32),
                 )
 
         def load_w(c):
@@ -103,10 +106,13 @@ def tile_relativemultiheadattention_pa_k_kernel(tc, pos_embed, W_r_words, W_r_sc
         for c in range(CHUNKS):
             for r in range(ROW_TILES):
                 x_tiles[(c, r)] = load_x(c, r)
-            if (c * STEP_GROUPS) % PART_GROUPS == 0:
-                load_scales((c * STEP_GROUPS) // PART_GROUPS)
+            if c * STEP_GROUPS in FIRST_OF_PART:
+                load_scales(PART_OF_GROUP[c * STEP_GROUPS])
             w_tiles[c] = load_w(c)
+            if c == 0:
+                nc.sync.dma_start(out=bias_row[0:1, :], in_=b_r.unsqueeze(0))
 
+        partial = const.tile([P, D_OUT], F32, name="partial")
         sums = []
         for r in range(ROW_TILES):
             total = sum_pool.tile([P, D_OUT], F32, name="sum%d" % r)
@@ -145,6 +151,10 @@ def tile_relativemultiheadattention_pa_k_kernel(tc, pos_embed, W_r_words, W_r_sc
                 quantised_banks.append((codes, scales))
             return quantised_banks
 
+        def plane_of_group(g):
+            part = PART_OF_GROUP[g]
+            return planes[part][:, g - FIRST_OF_PART[part], :]
+
         def multiply(step, quantised_banks):
             c, r = step
             for in_chunk in range(STEP_GROUPS):
@@ -156,14 +166,39 @@ def tile_relativemultiheadattention_pa_k_kernel(tc, pos_embed, W_r_words, W_r_sc
                     lhsT=codes[:, i * P : (i + 1) * P].bitcast(FP8X4),
                     lhsT_scale=scales[:, i * P : (i + 1) * P],
                     rhs=w_tiles[c][:, in_chunk, :].bitcast(FP4X4),
-                    rhs_scale=planes[g // PART_GROUPS][:, g % PART_GROUPS, :],
+                    rhs_scale=plane_of_group(g),
                     start=(g == 0),
-                    stop=(g == GROUPS - 1),
+                    stop=(g == LAST_SUMMED[r]),
                 )
-            if c == CHUNKS - 1:
+            if g == LAST_SUMMED[r] and r == LAST:
+                nc.vector.tensor_tensor(out=partial[:], in0=sums[r][:], in1=bias_all[:], op=mybir.AluOpType.add)
+            elif g == LAST_SUMMED[r]:
                 result = result_pool.tile([P, D_OUT], F32, name="result")
                 nc.vector.tensor_tensor(out=result[:], in0=sums[r][:], in1=bias_all[:], op=mybir.AluOpType.add)
                 nc.sync.dma_start(out=out_rows[r * P : (r + 1) * P, :], in_=result[:])
+
+        def multiply_end(quantised_banks):
+            for n0 in range(0, D_OUT, HALF):
+                half_bank = bank_pool.tile([P, D_OUT], F32, name="bank")
+                for m0 in range(0, HALF, P):
+                    for in_chunk in range(STEP_GROUPS):
+                        g = GROUPS - STEP_GROUPS + in_chunk
+                        codes, scales = quantised_banks[in_chunk // BANK_GROUPS]
+                        i = in_chunk % BANK_GROUPS
+                        nc.tensor.matmul_mx(
+                            out=half_bank[:, m0 : m0 + P],
+                            lhsT=codes[:, i * P : (i + 1) * P].bitcast(FP8X4),
+                            lhsT_scale=scales[:, i * P : (i + 1) * P],
+                            rhs=w_tiles[CHUNKS - 1][:, in_chunk, 2 * (n0 + m0) : 2 * (n0 + m0 + P)].bitcast(FP4X4),
+                            rhs_scale=plane_of_group(g)[:, n0 + m0 : n0 + m0 + P],
+                            start=(in_chunk == 0),
+                            stop=(in_chunk == STEP_GROUPS - 1),
+                        )
+                half = result_pool.tile([P, HALF], F32, name="half")
+                nc.vector.tensor_tensor(
+                    out=half[:], in0=half_bank[:, 0:HALF], in1=partial[:, n0 : n0 + HALF], op=mybir.AluOpType.add
+                )
+                nc.sync.dma_start(out=out_rows[LAST * P : (LAST + 1) * P, n0 : n0 + HALF], in_=half[:])
 
         in_order_of = {}
         quantised = {}
@@ -178,13 +213,13 @@ def tile_relativemultiheadattention_pa_k_kernel(tc, pos_embed, W_r_words, W_r_sc
                 for r in range(ROW_TILES):
                     in_order_of[(c + 1, r)] = sort_words((c + 1, r))
             quantised[(c, LAST)] = quantise_step(grouped_banks)
-            if c == 0:
+            if c == CHUNKS // 2:
                 bias_bank = bank_pool.tile([P, D_OUT], F32, name="bank")
                 nc.tensor.matmul(bias_bank[:], lhsT=ones[:], rhs=bias_row[:], start=True, stop=True)
                 bias_all = const.tile([P, D_OUT], F32, name="bias_all")
                 nc.scalar.copy(out=bias_all[:], in_=bias_bank[:])
-            else:
+            if c > 0:
                 multiply((c - 1, LAST), quantised[(c - 1, LAST)])
             for r in range(LAST):
                 multiply((c, r), quantised[(c, r)])
-        multiply((CHUNKS - 1, LAST), quantised[(CHUNKS - 1, LAST)])
+        multiply_end(quantised[(CHUNKS - 1, LAST)])

@@ -34,6 +34,8 @@ SCALE_PARTS = len(PART_GROUPS)
 FIRST_OF_PART = tuple(sum(PART_GROUPS[:part]) for part in range(SCALE_PARTS))
 PART_OF_GROUP = tuple(part for part in range(SCALE_PARTS) for g in range(PART_GROUPS[part]))
 HALF = D_OUT // 2
+BUSY_AT_START = 7
+BUSY_AFTER_STEP = 1
 LAST_SUMMED = (GROUPS - 1, GROUPS - 1, GROUPS - STEP_GROUPS - 1)
 
 FLOPS = 2 * ROWS * D_IN * D_OUT
@@ -57,6 +59,11 @@ def tile_relativemultiheadattention_pa_k_kernel(tc, pos_embed, W_r_words, W_r_sc
         sum_pool = ctx.enter_context(tc.psum_pool(name="sum", bufs=1))
         bank_pool = ctx.enter_context(tc.psum_pool(name="bank", bufs=PSUM_BANKS - ROW_TILES))
 
+        ones = const.tile([P, P], BF16, name="ones")
+        nothing = const.tile([P, D_OUT], BF16, name="nothing")
+        nc.gpsimd.memset(ones[:], 1.0)
+        nc.gpsimd.memset(nothing[:], 0.0)
+
         planes = []
         for part in range(SCALE_PARTS):
             plane = plane_pool.tile([P, PART_GROUPS[part], D_OUT], U8, align_bytes=64, name="plane")
@@ -71,9 +78,7 @@ def tile_relativemultiheadattention_pa_k_kernel(tc, pos_embed, W_r_words, W_r_sc
         nc.vector.tensor_copy(out=selector[:, 1, 0:127], in_=selector[:, 2, 0:127])
 
         bias_row = const.tile([P, D_OUT], BF16, name="bias_row")
-        ones = const.tile([P, P], BF16, name="ones")
         nc.vector.memset(bias_row[:], 0.0)
-        nc.vector.memset(ones[:], 1.0)
 
         def load_x(c, r):
             x_tile = x_pool.tile([P, STEP_GROUPS * K_PASS], BF16, name="x_tile")
@@ -117,6 +122,12 @@ def tile_relativemultiheadattention_pa_k_kernel(tc, pos_embed, W_r_words, W_r_sc
         for r in range(ROW_TILES):
             total = sum_pool.tile([P, D_OUT], F32, name="sum%d" % r)
             sums.append(total)
+
+        def keep_busy(count):
+            for i in range(count):
+                nc.tensor.matmul(sums[LAST][:], lhsT=ones[:], rhs=nothing[:], start=True, stop=True)
+
+        keep_busy(BUSY_AT_START)
 
         def sort_words(step):
             in_order = sorted_pool.tile([P, STEP_GROUPS, 2, P], F32, name="in_order")
@@ -207,6 +218,8 @@ def tile_relativemultiheadattention_pa_k_kernel(tc, pos_embed, W_r_words, W_r_sc
         for c in range(CHUNKS):
             for r in range(ROW_TILES):
                 grouped_banks = transpose_step((c, r), in_order_of[(c, r)])
+                if c == 0:
+                    keep_busy(BUSY_AFTER_STEP)
                 if r < LAST:
                     quantised[(c, r)] = quantise_step(grouped_banks)
             if c + 1 < CHUNKS:

@@ -59,6 +59,9 @@ def tile_relativemultiheadattention_pa_k_kernel(tc, pos_embed, W_r_words, W_r_sc
         sum_pool = ctx.enter_context(tc.psum_pool(name="sum", bufs=1))
         bank_pool = ctx.enter_context(tc.psum_pool(name="bank", bufs=PSUM_BANKS - ROW_TILES))
 
+        bias_row = const.tile([P, D_OUT], BF16, name="bias_row")
+        nc.gpsimd.memset(bias_row[:], 0.0)
+
         ones = const.tile([P, P], BF16, name="ones")
         nothing = const.tile([P, D_OUT], BF16, name="nothing")
         nc.gpsimd.memset(ones[:], 1.0)
@@ -72,13 +75,10 @@ def tile_relativemultiheadattention_pa_k_kernel(tc, pos_embed, W_r_words, W_r_sc
 
         selector = const.tile([P, ROW_TILES, P], F32, name="selector")
         make_identity(nc, selector[:, 2, :])
-        nc.vector.memset(selector[:, 0:2, :], 0.0)
+        nc.gpsimd.memset(selector[:, 0:2, :], 0.0)
         nc.vector.tensor_copy(out=selector[:, 0, 0:126], in_=selector[:, 2, 0:126])
         nc.vector.tensor_copy(out=selector[:, 0, 127:128], in_=selector[:, 2, 126:127])
         nc.vector.tensor_copy(out=selector[:, 1, 0:127], in_=selector[:, 2, 0:127])
-
-        bias_row = const.tile([P, D_OUT], BF16, name="bias_row")
-        nc.vector.memset(bias_row[:], 0.0)
 
         def load_x(c, r):
             x_tile = x_pool.tile([P, STEP_GROUPS * K_PASS], BF16, name="x_tile")
@@ -111,11 +111,11 @@ def tile_relativemultiheadattention_pa_k_kernel(tc, pos_embed, W_r_words, W_r_sc
         for c in range(CHUNKS):
             for r in range(ROW_TILES):
                 x_tiles[(c, r)] = load_x(c, r)
+                if c == 0 and r == 0:
+                    nc.sync.dma_start(out=bias_row[0:1, :], in_=b_r.unsqueeze(0))
             if c * STEP_GROUPS in FIRST_OF_PART:
                 load_scales(PART_OF_GROUP[c * STEP_GROUPS])
             w_tiles[c] = load_w(c)
-            if c == 0:
-                nc.sync.dma_start(out=bias_row[0:1, :], in_=b_r.unsqueeze(0))
 
         partial = const.tile([P, D_OUT], F32, name="partial")
         sums = []
@@ -128,6 +128,10 @@ def tile_relativemultiheadattention_pa_k_kernel(tc, pos_embed, W_r_words, W_r_sc
                 nc.tensor.matmul(sums[LAST][:], lhsT=ones[:], rhs=nothing[:], start=True, stop=True)
 
         keep_busy(BUSY_AT_START)
+        bias_bank = bank_pool.tile([P, D_OUT], F32, name="bank")
+        nc.tensor.matmul(bias_bank[:], lhsT=ones[:], rhs=bias_row[:], start=True, stop=True)
+        bias_all = const.tile([P, D_OUT], F32, name="bias_all")
+        nc.scalar.copy(out=bias_all[:], in_=bias_bank[:])
 
         def sort_words(step):
             in_order = sorted_pool.tile([P, STEP_GROUPS, 2, P], F32, name="in_order")
@@ -226,11 +230,6 @@ def tile_relativemultiheadattention_pa_k_kernel(tc, pos_embed, W_r_words, W_r_sc
                 for r in range(ROW_TILES):
                     in_order_of[(c + 1, r)] = sort_words((c + 1, r))
             quantised[(c, LAST)] = quantise_step(grouped_banks)
-            if c == CHUNKS // 2:
-                bias_bank = bank_pool.tile([P, D_OUT], F32, name="bank")
-                nc.tensor.matmul(bias_bank[:], lhsT=ones[:], rhs=bias_row[:], start=True, stop=True)
-                bias_all = const.tile([P, D_OUT], F32, name="bias_all")
-                nc.scalar.copy(out=bias_all[:], in_=bias_bank[:])
             if c > 0:
                 multiply((c - 1, LAST), quantised[(c - 1, LAST)])
             for r in range(LAST):

from contextlib import ExitStack

import concourse.mybir as mybir
from concourse.masks import make_identity

BF16 = mybir.dt.bfloat16
F32 = mybir.dt.float32
I32 = mybir.dt.int32
U32 = mybir.dt.uint32
U8 = mybir.dt.uint8
FP8X4 = mybir.dt.float8_e4m3fn_x4
FP4X4 = mybir.dt.float4_e2m1fn_x4

P = 128
PACK = 4
K_PASS = P * PACK
ROWS = 384
D_IN = 16384
D_OUT = 512
GROUPS = D_IN // K_PASS
ROW_TILES = ROWS // P
LAST = ROW_TILES - 1
WORDS = K_PASS // 2
PSUM_BANKS = 8

FIRST_ROW = (2, 129, 256)

STEP_GROUPS = 4
CHUNKS = GROUPS // STEP_GROUPS
BANK_GROUPS = 2
STEP_BANKS = STEP_GROUPS // BANK_GROUPS
PART_GROUPS = (4, 8, 8, 8, 4)
SCALE_PARTS = len(PART_GROUPS)
FIRST_OF_PART = tuple(sum(PART_GROUPS[:part]) for part in range(SCALE_PARTS))
PART_OF_GROUP = tuple(part for part in range(SCALE_PARTS) for g in range(PART_GROUPS[part]))
HALF = D_OUT // 2
BUSY_AT_START = 7
BUSY_AFTER_STEP = 1
LAST_SUMMED = (GROUPS - 1, GROUPS - 1, GROUPS - STEP_GROUPS - 1)

FLOPS = 2 * ROWS * D_IN * D_OUT


def tile_relativemultiheadattention_pa_k_kernel(tc, pos_embed, W_r_words, W_r_scales, b_r, out):
    nc = tc.nc
    x_rows = pos_embed.flatten_outer_dims()
    out_rows = out.flatten_outer_dims()

    with ExitStack() as ctx:
        ctx.enter_context(tc.manual_schedule())
        const = ctx.enter_context(tc.tile_pool(name="const", bufs=1))
        x_pool = ctx.enter_context(tc.tile_pool(name="x", bufs=CHUNKS * ROW_TILES))
        w_pool = ctx.enter_context(tc.tile_pool(name="w", bufs=CHUNKS))
        plane_pool = ctx.enter_context(tc.tile_pool(name="plane", bufs=SCALE_PARTS))
        sorted_pool = ctx.enter_context(tc.tile_pool(name="sorted", bufs=2 * ROW_TILES))
        grouped_pool = ctx.enter_context(tc.tile_pool(name="grouped", bufs=ROW_TILES * STEP_BANKS))
        code_pool = ctx.enter_context(tc.tile_pool(name="code", bufs=2 * ROW_TILES * STEP_BANKS))
        result_pool = ctx.enter_context(tc.tile_pool(name="result", bufs=ROW_TILES))
        sum_pool = ctx.enter_context(tc.psum_pool(name="sum", bufs=1))
        bank_pool = ctx.enter_context(tc.psum_pool(name="bank", bufs=PSUM_BANKS - ROW_TILES))

        bias_row = const.tile([P, D_OUT], BF16, name="bias_row")
        nc.gpsimd.memset(bias_row[:], 0.0)

        ones = const.tile([P, P], BF16, name="ones")
        nothing = const.tile([P, D_OUT], BF16, name="nothing")
        nc.gpsimd.memset(ones[:], 1.0)
        nc.gpsimd.memset(nothing[:], 0.0)

        planes = []
        for part in range(SCALE_PARTS):
            plane = plane_pool.tile([P, PART_GROUPS[part], D_OUT], U8, align_bytes=64, name="plane")
            nc.vector.memset(plane[:].rearrange("p g n -> p (g n)").bitcast(I32), 0)
            planes.append(plane)

        selector = const.tile([P, ROW_TILES, P], F32, name="selector")
        make_identity(nc, selector[:, 2, :])
        nc.gpsimd.memset(selector[:, 0:2, :], 0.0)
        nc.vector.tensor_copy(out=selector[:, 0, 0:126], in_=selector[:, 2, 0:126])
        nc.vector.tensor_copy(out=selector[:, 0, 127:128], in_=selector[:, 2, 126:127])
        nc.vector.tensor_copy(out=selector[:, 1, 0:127], in_=selector[:, 2, 0:127])

        def load_x(c, r):
            x_tile = x_pool.tile([P, STEP_GROUPS * K_PASS], BF16, name="x_tile")
            k0 = c * STEP_GROUPS * K_PASS
            nc.sync.dma_start(
                out=x_tile[:],
                in_=x_rows[FIRST_ROW[r] : FIRST_ROW[r] + P, k0 : k0 + STEP_GROUPS * K_PASS],
            )
            return x_tile

        def load_scales(part):
            g0 = FIRST_OF_PART[part]
            for t in range(4):
                nc.sync.dma_start(
                    out=planes[part][t : P : 32, :, :].bitcast(I32),
                    in_=W_r_scales[g0 : g0 + PART_GROUPS[part], t : 16 : 4, :].rearrange("g q n -> q g n").bitcast(I32),
                )

        def load_w(c):
            w_tile = w_pool.tile([P, STEP_GROUPS, 2 * D_OUT], U8, align_bytes=64, name="w_tile")
            g0 = c * STEP_GROUPS
            nc.sync.dma_start(
                out=w_tile[:].bitcast(I32),
                in_=W_r_words[g0 : g0 + STEP_GROUPS].rearrange("g p b -> p g b").bitcast(I32),
            )
            return w_tile

        x_tiles = {}
        w_tiles = {}
        for c in range(CHUNKS):
            for r in range(ROW_TILES):
                x_tiles[(c, r)] = load_x(c, r)
                if c == 0 and r == 0:
                    nc.sync.dma_start(out=bias_row[0:1, :], in_=b_r.unsqueeze(0))
            if c * STEP_GROUPS in FIRST_OF_PART:
                load_scales(PART_OF_GROUP[c * STEP_GROUPS])
            w_tiles[c] = load_w(c)

        partial = const.tile([P, D_OUT], F32, name="partial")
        sums = []
        for r in range(ROW_TILES):
            total = sum_pool.tile([P, D_OUT], F32, name="sum%d" % r)
            sums.append(total)

        def keep_busy(count):
            for i in range(count):
                nc.tensor.matmul(sums[LAST][:], lhsT=ones[:], rhs=nothing[:], start=True, stop=True)

        keep_busy(BUSY_AT_START)
        bias_bank = bank_pool.tile([P, D_OUT], F32, name="bank")
        nc.tensor.matmul(bias_bank[:], lhsT=ones[:], rhs=bias_row[:], start=True, stop=True)
        bias_all = const.tile([P, D_OUT], F32, name="bias_all")
        nc.scalar.copy(out=bias_all[:], in_=bias_bank[:])

        def sort_words(step):
            in_order = sorted_pool.tile([P, STEP_GROUPS, 2, P], F32, name="in_order")
            nc.vector.tensor_copy(
                out=in_order[:].rearrange("r i u p -> r i p u"),
                in_=x_tiles[step][:].bitcast(F32).rearrange("r (i p u) -> r i p u", i=STEP_GROUPS, u=2),
            )
            return in_order

        def transpose_step(step, in_order):
            r = step[1]
            grouped_banks = []
            for h in range(STEP_BANKS):
                bank = bank_pool.tile([P, BANK_GROUPS, 2, P], F32, name="bank")
                for i in range(BANK_GROUPS):
                    for u in range(2):
                        nc.tensor.transpose(bank[:, i, u, :], in_order[:, h * BANK_GROUPS + i, u, :], selector[:, r, :])
                grouped = grouped_pool.tile([P, BANK_GROUPS * P * PACK], BF16, align_bytes=64, name="grouped")
                nc.scalar.copy(
                    out=grouped[:].bitcast(F32).rearrange("p (i j u) -> p i j u", i=BANK_GROUPS, u=2),
                    in_=bank[:].rearrange("p i u j -> p i j u"),
                )
                grouped_banks.append(grouped)
            return grouped_banks

        def quantise_step(grouped_banks):
            quantised_banks = []
            for grouped in grouped_banks:
                codes = code_pool.tile([P, BANK_GROUPS * P], U32, align_bytes=64, name="codes")
                scales = code_pool.tile([P, BANK_GROUPS * P], U8, align_bytes=64, name="scales")
                nc.vector.quantize_mx(out=codes[:].bitcast(FP8X4), scales=scales[:], in_=grouped[:])
                quantised_banks.append((codes, scales))
            return quantised_banks

        def plane_of_group(g):
            part = PART_OF_GROUP[g]
            return planes[part][:, g - FIRST_OF_PART[part], :]

        def multiply(step, quantised_banks):
            c, r = step
            for in_chunk in range(STEP_GROUPS):
                g = c * STEP_GROUPS + in_chunk
                codes, scales = quantised_banks[in_chunk // BANK_GROUPS]
                i = in_chunk % BANK_GROUPS
                nc.tensor.matmul_mx(
                    out=sums[r][:],
                    lhsT=codes[:, i * P : (i + 1) * P].bitcast(FP8X4),
                    lhsT_scale=scales[:, i * P : (i + 1) * P],
                    rhs=w_tiles[c][:, in_chunk, :].bitcast(FP4X4),
                    rhs_scale=plane_of_group(g),
                    start=(g == 0),
                    stop=(g == LAST_SUMMED[r]),
                )
            if g == LAST_SUMMED[r] and r == LAST:
                nc.vector.tensor_tensor(out=partial[:], in0=sums[r][:], in1=bias_all[:], op=mybir.AluOpType.add)
            elif g == LAST_SUMMED[r]:
                result = result_pool.tile([P, D_OUT], F32, name="result")
                nc.vector.tensor_tensor(out=result[:], in0=sums[r][:], in1=bias_all[:], op=mybir.AluOpType.add)
                nc.sync.dma_start(out=out_rows[r * P : (r + 1) * P, :], in_=result[:])

        def multiply_end(quantised_banks):
            for n0 in range(0, D_OUT, HALF):
                half_bank = bank_pool.tile([P, D_OUT], F32, name="bank")
                for m0 in range(0, HALF, P):
                    for in_chunk in range(STEP_GROUPS):
                        g = GROUPS - STEP_GROUPS + in_chunk
                        codes, scales = quantised_banks[in_chunk // BANK_GROUPS]
                        i = in_chunk % BANK_GROUPS
                        nc.tensor.matmul_mx(
                            out=half_bank[:, m0 : m0 + P],
                            lhsT=codes[:, i * P : (i + 1) * P].bitcast(FP8X4),
                            lhsT_scale=scales[:, i * P : (i + 1) * P],
                            rhs=w_tiles[CHUNKS - 1][:, in_chunk, 2 * (n0 + m0) : 2 * (n0 + m0 + P)].bitcast(FP4X4),
                            rhs_scale=plane_of_group(g)[:, n0 + m0 : n0 + m0 + P],
                            start=(in_chunk == 0),
                            stop=(in_chunk == STEP_GROUPS - 1),
                        )
                half = result_pool.tile([P, HALF], F32, name="half")
                nc.vector.tensor_tensor(
                    out=half[:], in0=half_bank[:, 0:HALF], in1=partial[:, n0 : n0 + HALF], op=mybir.AluOpType.add
                )
                nc.sync.dma_start(out=out_rows[LAST * P : (LAST + 1) * P, n0 : n0 + HALF], in_=half[:])

        in_order_of = {}
        quantised = {}
        for r in range(ROW_TILES):
            in_order_of[(0, r)] = sort_words((0, r))
        for c in range(CHUNKS):
            for r in range(ROW_TILES):
                grouped_banks = transpose_step((c, r), in_order_of[(c, r)])
                if c == 0:
                    keep_busy(BUSY_AFTER_STEP)
                if r < LAST:
                    quantised[(c, r)] = quantise_step(grouped_banks)
            if c + 1 < CHUNKS:
                for r in range(ROW_TILES):
                    in_order_of[(c + 1, r)] = sort_words((c + 1, r))
            quantised[(c, LAST)] = quantise_step(grouped_banks)
            if c > 0:
                multiply((c - 1, LAST), quantised[(c - 1, LAST)])
            for r in range(LAST):
                multiply((c, r), quantised[(c, r)])
        multiply_end(quantised[(CHUNKS - 1, LAST)])
